import numpy as np
import ml_dtypes


def mxq(x, axis, fmt="e4m3"):
    dtype, down = {"e4m3": (ml_dtypes.float8_e4m3fn, 7), "e5m2": (ml_dtypes.float8_e5m2, 14)}[fmt]
    v = np.moveaxis(np.asarray(x, np.float32).astype(ml_dtypes.bfloat16).astype(np.float64), axis, -1)
    blocks = v.reshape(v.shape[:-1] + (-1, 32))
    amax = np.abs(blocks).max(-1, keepdims=True)
    byte = np.maximum(np.where(amax > 0, np.frexp(amax)[1] - 1 + 127, 0) - down, 1)
    scale = np.exp2(byte - 127.0)
    codes = (blocks / scale).astype(np.float32).astype(dtype).astype(np.float64)
    return np.moveaxis((codes * scale).reshape(v.shape), -1, axis)


WIDE = False


def mx_kscale(k):
    if not WIDE:
        return np.ones(k)
    levels = np.array([10, -10, 5, -5, 0])
    if k % 512:
        return np.exp2(np.random.permutation(np.resize(levels, k // 32))).repeat(32)
    a = np.empty((k // 512, 16))
    for p in range(k // 512):
        a[p, :8] = np.random.permutation(np.resize(levels, 8))
        for g in range(8):
            far = levels[np.abs(levels - a[p, g]) >= 10]
            a[p, g + 8] = far[np.random.randint(len(far))]
    return np.exp2(a.ravel()).repeat(32)


BF16 = ml_dtypes.bfloat16


def bf(x):
    return np.asarray(x, np.float32).astype(BF16)


def f64(x):
    return np.asarray(x).astype(np.float64)


B, HALF, MID = 512, 512, 2048
D = 2 * HALF


def setup_inputs():
    s, t = mx_kscale(MID), mx_kscale(MID)
    return {"x": bf(np.random.standard_normal((B, D))),
            "h3": bf(np.maximum(np.random.standard_normal((B, MID)), 0.0) * s),
            "W4": bf(np.random.standard_normal((MID, MID)) * np.sqrt(2.0 / MID) / s[:, None] * t),
            "b4": bf(np.random.standard_normal(MID) * 0.2 * t),
            "W5": bf(np.random.standard_normal((MID, HALF)) * np.sqrt(2.0 / MID) / t[:, None]),
            "b5": bf(np.random.standard_normal(HALF) * 0.2)}


def reference(x, h3, W4, b4, W5, b5):
    x = f64(x)
    even = x[:, 0::2]
    odd = x[:, 1::2]
    h4 = np.maximum((mxq(f64(h3), 1, "e4m3") @ mxq(f64(W4), 0, "e4m3")) + f64(b4), 0.0)
    m = (mxq(h4, 1, "e4m3") @ mxq(f64(W5), 0, "e4m3")) + f64(b5)
    transformed = even + m
    return np.stack([transformed, odd], axis=2).reshape(B, -1)

@@ -1,0 +1,297 @@
+from contextlib import ExitStack
+
+import concourse.mybir as mybir
+from concourse.masks import make_identity
+
+F32 = mybir.dt.float32
+BF16 = mybir.dt.bfloat16
+U32 = mybir.dt.uint32
+U8 = mybir.dt.uint8
+FP8X4 = mybir.dt.float8_e4m3fn_x4
+ACT = mybir.ActivationFunctionType
+ALU = mybir.AluOpType
+
+P = 128
+B = 512
+MID = 2048
+HALF = 512
+KP = 512
+NG = MID // KP
+NBT = B // P
+
+FLOPS = 2 * B * MID * MID + 2 * B * MID * HALF
+
+LOOKAHEAD = 12
+NV_W = 264
+MH = 2
+
+
+def regroup(nc, dst, src, width, nv):
+    nc.vector.tensor_copy(
+        out=dst[:, 0:nv, :].rearrange("p (c i) t -> p c t i", i=4),
+        in_=src[:, :, 0:nv].rearrange("p t (c i) -> p c t i", i=4),
+    )
+    if nv < width:
+        nc.scalar.copy(
+            out=dst[:, nv:width, :].rearrange("p (c i) t -> p c t i", i=4),
+            in_=src[:, :, nv:width].rearrange("p t (c i) -> p c t i", i=4),
+        )
+
+
+def regroup_w4(nc, dst, src, nv):
+    d = dst[:].rearrange("p t (a b) j -> p t a j b", b=MH)
+    s = src[:].rearrange("p j (a b t) -> p t a j b", b=MH, t=4)
+    cut = nv // (4 * MH)
+    nc.vector.tensor_copy(out=d[:, :, 0:cut], in_=s[:, :, 0:cut])
+    nc.scalar.copy(out=d[:, :, cut:], in_=s[:, :, cut:])
+
+
+def tile_additivecoupling_pa_kernel(tc, x, h3, W4, b4, W5, b5, out):
+    nc = tc.nc
+    with ExitStack() as ctx:
+        const = ctx.enter_context(tc.tile_pool(name="const", bufs=1))
+        keep = ctx.enter_context(tc.tile_pool(name="keep", bufs=1))
+        raw4 = ctx.enter_context(tc.tile_pool(name="raw4", bufs=LOOKAHEAD))
+        grp = ctx.enter_context(tc.tile_pool(name="grp", bufs=4))
+        cod4 = ctx.enter_context(tc.tile_pool(name="cod4", bufs=6))
+        h4pool = ctx.enter_context(tc.tile_pool(name="h4pool", bufs=2))
+        opool = ctx.enter_context(tc.tile_pool(name="opool", bufs=8))
+        psa = ctx.enter_context(tc.psum_pool(name="psa", bufs=8))
+
+        ident = const.tile([P, P], F32, name="ident")
+        make_identity(nc, ident[:])
+        identb = const.tile([P, P], BF16, name="identb")
+        nc.vector.tensor_copy(out=identb[:], in_=ident[:])
+
+        brow = const.tile([P, 512], BF16, name="brow")
+        nc.vector.memset(brow[:], 0.0)
+        nc.sync.dma_start(out=brow[0:4, :], in_=b4.rearrange("(r c) -> r c", c=512))
+        nc.sync.dma_start(out=brow[4:5, :], in_=b5.rearrange("(r c) -> r c", c=512))
+
+        h3r = []
+        for bt in range(NBT):
+            t_ = keep.tile([P, MID], BF16, name="h3r%d" % bt)
+            nc.sync.dma_start(out=t_[:], in_=h3[bt * P : (bt + 1) * P, :])
+            h3r.append(t_)
+
+        w4r = {}
+
+        def load_w4(i):
+            c2, g = divmod(i, NG)
+            r = raw4.tile([P, 4, KP], BF16, name="w4r", tag="w4r")
+            nc.sync.dma_start(
+                out=r[:],
+                in_=W4[g * KP : (g + 1) * KP, c2 * KP : (c2 + 1) * KP].rearrange("(p j) c -> p j c", j=4),
+            )
+            w4r[i] = r
+
+        for i in range(LOOKAHEAD):
+            load_w4(i)
+
+        w5r = []
+        xr = []
+
+        def load_tail():
+            for c in range(NG):
+                t_ = keep.tile([P, 4, HALF], BF16, name="w5r%d" % c)
+                nc.sync.dma_start(
+                    out=t_[:], in_=W5[c * KP : (c + 1) * KP, :].rearrange("(p t) j -> p t j", t=4)
+                )
+                w5r.append(t_)
+            for bt in range(NBT):
+                t_ = keep.tile([P, 2 * HALF], BF16, name="xr%d" % bt)
+                nc.sync.dma_start(out=t_[:], in_=x[bt * P : (bt + 1) * P, :])
+                xr.append(t_)
+
+        h3g = keep.tile([P, NG, B, 2], F32, name="h3g", align_bytes=64)
+        h3c = keep.tile([P, NG, B], U32, name="h3c", align_bytes=64)
+        h3s = keep.tile([P, NG, B], U8, name="h3s", align_bytes=64)
+        n_exit = 0
+        for bt in range(NBT):
+            words = h3r[bt][:].bitcast(F32)
+            for gp in range(2):
+                pt = psa.tile([P, 2, 2, P], F32, name="pt", tag="a")
+                for gg in range(2):
+                    for u in range(2):
+                        w0 = (2 * gp + gg) * 256
+                        nc.tensor.transpose(pt[:, gg, u, :], words[:, w0 + u : w0 + 256 : 2], ident[:])
+                dst = h3g[:, 2 * gp : 2 * gp + 2, bt * P : (bt + 1) * P, :]
+                src = pt[:].rearrange("p g u b -> p g b u")
+                if n_exit % 2 == 0:
+                    nc.scalar.copy(out=dst, in_=src)
+                else:
+                    nc.vector.tensor_copy(out=dst, in_=src)
+                n_exit += 1
+        for g in range(NG):
+            nc.vector.quantize_mx(
+                out=h3c[:, g, :].bitcast(FP8X4),
+                scales=h3s[:, g, :],
+                in_=h3g[:, g, :, :].rearrange("p b u -> p (b u)").bitcast(BF16),
+            )
+
+        browf = const.tile([P, 512], F32, name="browf")
+        nc.vector.tensor_copy(out=browf[:], in_=brow[:])
+        pb = psa.tile([P, 4, P], F32, name="pb", tag="a")
+        pb5 = psa.tile([P, 4, P], F32, name="pb5", tag="a")
+        for t in range(4):
+            nc.tensor.transpose(pb[:, t, :], browf[:, t : 512 : 4], ident[:])
+            nc.tensor.transpose(pb5[:, t, :], browf[:, t * P : (t + 1) * P], ident[:])
+        bias = const.tile([P, 4, 4], F32, name="bias")
+        nc.vector.tensor_copy(out=bias[:], in_=pb[:, :, 0:4].rearrange("p t c -> p c t"))
+        bias5 = const.tile([P, 4], F32, name="bias5")
+        nc.vector.tensor_copy(out=bias5[:], in_=pb5[:, :, 4])
+
+        w4g = {}
+        ps1 = {}
+        h4p = {}
+        h4g = {}
+        h4c = [keep.tile([P, B], U32, name="h4c%d" % c, align_bytes=64) for c in range(NG)]
+        h4s = [keep.tile([P, B], U8, name="h4s%d" % c, align_bytes=64) for c in range(NG)]
+
+        def stage_a(i):
+            g_ = grp.tile([P, 4, P, 4], BF16, name="wg", tag="g", align_bytes=64)
+            regroup_w4(nc, g_, w4r[i], NV_W)
+            w4g[i] = g_
+
+        def stage_b(i):
+            c2, g = divmod(i, NG)
+            codes = cod4.tile([P, KP], U32, name="w4c", tag="w4c", align_bytes=64)
+            scales = cod4.tile([P, KP], U8, name="w4s", tag="w4s", align_bytes=64)
+            nc.vector.quantize_mx(
+                out=codes[:].bitcast(FP8X4),
+                scales=scales[:],
+                in_=w4g[i][:].rearrange("p t m j -> p (t m j)"),
+            )
+            for t in range(4):
+                if g == 0:
+                    ps1[t] = psa.tile([P, B], F32, name="ps1", tag="a")
+                nc.tensor.matmul_mx(
+                    out=ps1[t][:],
+                    lhsT=codes[:, t * P : (t + 1) * P].bitcast(FP8X4),
+                    lhsT_scale=scales[:, t * P : (t + 1) * P],
+                    rhs=h3c[:, g, :].bitcast(FP8X4),
+                    rhs_scale=h3s[:, g, :],
+                    start=(g == 0),
+                    stop=(g == NG - 1),
+                )
+
+        def stage_c(c2, on_vector):
+            hp = h4pool.tile([P, 4, B], BF16, name="h4p", tag="h4p")
+            for t in range(4):
+                col = bias[:, c2, t : t + 1]
+                if t in on_vector:
+                    nc.vector.tensor_scalar(
+                        out=hp[:, t, :], in0=ps1[t][:], scalar1=col, scalar2=0.0, op0=ALU.add, op1=ALU.max
+                    )
+                else:
+                    nc.scalar.activation(out=hp[:, t, :], in_=ps1[t][:], func=ACT.Relu, bias=col, scale=1.0)
+            h4p[c2] = hp
+
+        def stage_d(c2, nv):
+            hg = h4pool.tile([P, B, 4], BF16, name="h4g", tag="h4g", align_bytes=64)
+            regroup(nc, hg, h4p[c2], B, nv)
+            h4g[c2] = hg
+
+        def stage_e(c2):
+            nc.vector.quantize_mx(
+                out=h4c[c2][:].bitcast(FP8X4),
+                scales=h4s[c2][:],
+                in_=h4g[c2][:].rearrange("p b t -> p (b t)"),
+            )
+
+        for i in range(4 * NG + 1):
+            if i < 4 * NG:
+                stage_a(i)
+                if i + LOOKAHEAD < 4 * NG:
+                    load_w4(i + LOOKAHEAD)
+                if i + LOOKAHEAD == 4 * NG - 1:
+                    load_tail()
+            if i >= 6 and i % 4 == 2:
+                stage_d(i // 4 - 1, B)
+            if i >= 1:
+                stage_b(i - 1)
+                if (i - 1) % 4 == 3:
+                    last = i == 4 * NG
+                    stage_c((i - 1) // 4, (1, 3) if last else ())
+            if i >= 7 and i % 4 == 3:
+                stage_e(i // 4 - 1)
+
+        w5c = keep.tile([P, NG, HALF], U32, name="w5c", align_bytes=64)
+        w5s = keep.tile([P, NG, HALF], U8, name="w5s", align_bytes=64)
+        w5g = {}
+
+        def stage_a5(c):
+            g_ = grp.tile([P, HALF, 4], BF16, name="wg5", tag="g", align_bytes=64)
+            regroup(nc, g_, w5r[c], HALF, NV_W)
+            w5g[c] = g_
+
+        def stage_q5(c):
+            nc.vector.quantize_mx(
+                out=w5c[:, c, :].bitcast(FP8X4),
+                scales=w5s[:, c, :],
+                in_=w5g[c][:].rearrange("p c t -> p (c t)"),
+            )
+
+        stage_a5(0)
+        stage_a5(1)
+        stage_d(3, 320)
+        stage_q5(0)
+        stage_a5(2)
+        stage_e(3)
+        stage_q5(1)
+        stage_a5(3)
+        stage_q5(2)
+        stage_q5(3)
+
+        acc = [psa.tile([P, B], F32, name="acc%d" % jt, tag="a") for jt in range(4)]
+        for c in range(NG):
+            for jt in range(4):
+                nc.tensor.matmul_mx(
+                    out=acc[jt][:],
+                    lhsT=w5c[:, c, jt * P : (jt + 1) * P].bitcast(FP8X4),
+                    lhsT_scale=w5s[:, c, jt * P : (jt + 1) * P],
+                    rhs=h4c[c][:].bitcast(FP8X4),
+                    rhs_scale=h4s[c][:],
+                    start=(c == 0),
+                    stop=(c == NG - 1),
+                )
+
+        zt = []
+        for jt in range(4):
+            z = keep.tile([P, B], F32, name="zt%d" % jt)
+            col = bias5[:, jt : jt + 1]
+            if jt % 2 == 0:
+                nc.scalar.activation(out=z[:], in_=acc[jt][:], func=ACT.Identity, bias=col, scale=1.0)
+            else:
+                nc.vector.tensor_scalar(out=z[:], in0=acc[jt][:], scalar1=col, scalar2=None, op0=ALU.add)
+            zt.append(z)
+        n_exit = 0
+        for ch in range(2):
+            for bt in range(NBT):
+                f = psa.tile([P, 2, 256], F32, name="f", tag="a")
+                nc.tensor.matmul(
+                    out=f[:],
+                    lhsT=identb[:],
+                    rhs=xr[bt][:, ch * 512 : (ch + 1) * 512].rearrange("p (j e) -> p e j", e=2),
+                    start=True,
+                    stop=False,
+                )
+                for r in range(2):
+                    nc.tensor.matmul(
+                        out=f[:, 0, r * P : (r + 1) * P],
+                        lhsT=zt[2 * ch + r][:, bt * P : (bt + 1) * P],
+                        rhs=ident[:],
+                        is_transpose=True,
+                        start=False,
+                        stop=(r == 1),
+                    )
+                o = opool.tile([P, 256, 2], F32, name="o", tag="o")
+                if n_exit % 2 == 0:
+                    nc.scalar.copy(out=o[:], in_=f[:].rearrange("p e j -> p j e"))
+                else:
+                    nc.vector.tensor_copy(out=o[:], in_=f[:].rearrange("p e j -> p j e"))
+                n_exit += 1
+                nc.sync.dma_start(
+                    out=out[bt * P : (bt + 1) * P, ch * 512 : (ch + 1) * 512],
+                    in_=o[:].rearrange("p j e -> p (j e)"),
+                )

@@ -21,8 +21,11 @@ NBT = B // P
 
 FLOPS = 2 * B * MID * MID + 2 * B * MID * HALF
 
-LOOKAHEAD = 12
-NV_W = 264
+HEAD = 2
+NCH = 16
+HJ = HALF // 2
+NV_W5 = HJ // 2
+NV_W = 240
 MH = 2
 
 
@@ -51,7 +54,7 @@ def tile_additivecoupling_pa_kernel(tc, x, h3, W4, b4, W5, b5, out):
     with ExitStack() as ctx:
         const = ctx.enter_context(tc.tile_pool(name="const", bufs=1))
         keep = ctx.enter_context(tc.tile_pool(name="keep", bufs=1))
-        raw4 = ctx.enter_context(tc.tile_pool(name="raw4", bufs=LOOKAHEAD))
+        raw4 = ctx.enter_context(tc.tile_pool(name="raw4", bufs=NCH))
         grp = ctx.enter_context(tc.tile_pool(name="grp", bufs=4))
         cod4 = ctx.enter_context(tc.tile_pool(name="cod4", bufs=6))
         h4pool = ctx.enter_context(tc.tile_pool(name="h4pool", bufs=2))
@@ -60,21 +63,14 @@ def tile_additivecoupling_pa_kernel(tc, x, h3, W4, b4, W5, b5, out):
 
         ident = const.tile([P, P], F32, name="ident")
         make_identity(nc, ident[:])
+        ctx.enter_context(tc.manual_schedule())
+        brow = const.tile([P, 512], BF16, name="brow")
+        nc.vector.memset(brow[:], 0.0)
         identb = const.tile([P, P], BF16, name="identb")
         nc.vector.tensor_copy(out=identb[:], in_=ident[:])
 
-        brow = const.tile([P, 512], BF16, name="brow")
-        nc.vector.memset(brow[:], 0.0)
-        nc.sync.dma_start(out=brow[0:4, :], in_=b4.rearrange("(r c) -> r c", c=512))
-        nc.sync.dma_start(out=brow[4:5, :], in_=b5.rearrange("(r c) -> r c", c=512))
-
-        h3r = []
-        for bt in range(NBT):
-            t_ = keep.tile([P, MID], BF16, name="h3r%d" % bt)
-            nc.sync.dma_start(out=t_[:], in_=h3[bt * P : (bt + 1) * P, :])
-            h3r.append(t_)
-
-        w4r = {}
+        raw = []
+        raw5 = []
 
         def load_w4(i):
             c2, g = divmod(i, NG)
@@ -83,31 +79,36 @@ def tile_additivecoupling_pa_kernel(tc, x, h3, W4, b4, W5, b5, out):
                 out=r[:],
                 in_=W4[g * KP : (g + 1) * KP, c2 * KP : (c2 + 1) * KP].rearrange("(p j) c -> p j c", j=4),
             )
-            w4r[i] = r
+            raw.append(r)
 
-        for i in range(LOOKAHEAD):
+        for i in range(HEAD):
             load_w4(i)
-
-        w5r = []
+        h3r = []
+        for bt in range(NBT):
+            t_ = keep.tile([P, MID], BF16, name="h3r%d" % bt)
+            nc.sync.dma_start(out=t_[:], in_=h3[bt * P : (bt + 1) * P, :])
+            h3r.append(t_)
+        nc.sync.dma_start(out=brow[0:4, :], in_=b4.rearrange("(r c) -> r c", c=512))
+        nc.sync.dma_start(out=brow[4:5, :], in_=b5.rearrange("(r c) -> r c", c=512))
+        for i in range(HEAD, NCH):
+            load_w4(i)
+        for c in range(NG):
+            r = keep.tile([P, 4, HALF], BF16, name="w5r%d" % c)
+            nc.sync.dma_start(
+                out=r[:], in_=W5[c * KP : (c + 1) * KP, :].rearrange("(p t) j -> p t j", t=4)
+            )
+            raw5.append(r)
         xr = []
-
-        def load_tail():
-            for c in range(NG):
-                t_ = keep.tile([P, 4, HALF], BF16, name="w5r%d" % c)
-                nc.sync.dma_start(
-                    out=t_[:], in_=W5[c * KP : (c + 1) * KP, :].rearrange("(p t) j -> p t j", t=4)
-                )
-                w5r.append(t_)
-            for bt in range(NBT):
-                t_ = keep.tile([P, 2 * HALF], BF16, name="xr%d" % bt)
-                nc.sync.dma_start(out=t_[:], in_=x[bt * P : (bt + 1) * P, :])
-                xr.append(t_)
+        for bt in range(NBT):
+            t_ = keep.tile([P, 2 * HALF], BF16, name="xr%d" % bt)
+            nc.sync.dma_start(out=t_[:], in_=x[bt * P : (bt + 1) * P, :])
+            xr.append(t_)
 
         h3g = keep.tile([P, NG, B, 2], F32, name="h3g", align_bytes=64)
         h3c = keep.tile([P, NG, B], U32, name="h3c", align_bytes=64)
         h3s = keep.tile([P, NG, B], U8, name="h3s", align_bytes=64)
-        n_exit = 0
-        for bt in range(NBT):
+
+        def turn_h3(bt):
             words = h3r[bt][:].bitcast(F32)
             for gp in range(2):
                 pt = psa.tile([P, 2, 2, P], F32, name="pt", tag="a")
@@ -117,181 +118,239 @@ def tile_additivecoupling_pa_kernel(tc, x, h3, W4, b4, W5, b5, out):
                         nc.tensor.transpose(pt[:, gg, u, :], words[:, w0 + u : w0 + 256 : 2], ident[:])
                 dst = h3g[:, 2 * gp : 2 * gp + 2, bt * P : (bt + 1) * P, :]
                 src = pt[:].rearrange("p g u b -> p g b u")
-                if n_exit % 2 == 0:
+                if gp == 0:
                     nc.scalar.copy(out=dst, in_=src)
                 else:
                     nc.vector.tensor_copy(out=dst, in_=src)
-                n_exit += 1
-        for g in range(NG):
+
+        def quant_h3(g):
             nc.vector.quantize_mx(
                 out=h3c[:, g, :].bitcast(FP8X4),
                 scales=h3s[:, g, :],
                 in_=h3g[:, g, :, :].rearrange("p b u -> p (b u)").bitcast(BF16),
             )
 
-        browf = const.tile([P, 512], F32, name="browf")
-        nc.vector.tensor_copy(out=browf[:], in_=brow[:])
-        pb = psa.tile([P, 4, P], F32, name="pb", tag="a")
-        pb5 = psa.tile([P, 4, P], F32, name="pb5", tag="a")
-        for t in range(4):
-            nc.tensor.transpose(pb[:, t, :], browf[:, t : 512 : 4], ident[:])
-            nc.tensor.transpose(pb5[:, t, :], browf[:, t * P : (t + 1) * P], ident[:])
-        bias = const.tile([P, 4, 4], F32, name="bias")
-        nc.vector.tensor_copy(out=bias[:], in_=pb[:, :, 0:4].rearrange("p t c -> p c t"))
-        bias5 = const.tile([P, 4], F32, name="bias5")
-        nc.vector.tensor_copy(out=bias5[:], in_=pb5[:, :, 4])
-
-        w4g = {}
+        grouped = {}
+        codes = {}
         ps1 = {}
         h4p = {}
         h4g = {}
         h4c = [keep.tile([P, B], U32, name="h4c%d" % c, align_bytes=64) for c in range(NG)]
         h4s = [keep.tile([P, B], U8, name="h4s%d" % c, align_bytes=64) for c in range(NG)]
+        w5c = [keep.tile([P, HALF], U32, name="w5c%d" % c, align_bytes=64) for c in range(NG)]
+        w5s = [keep.tile([P, HALF], U8, name="w5s%d" % c, align_bytes=64) for c in range(NG)]
 
-        def stage_a(i):
+        def group_w(i):
             g_ = grp.tile([P, 4, P, 4], BF16, name="wg", tag="g", align_bytes=64)
-            regroup_w4(nc, g_, w4r[i], NV_W)
-            w4g[i] = g_
+            regroup_w4(nc, g_, raw[i], NV_W)
+            grouped[i] = g_
 
-        def stage_b(i):
-            c2, g = divmod(i, NG)
-            codes = cod4.tile([P, KP], U32, name="w4c", tag="w4c", align_bytes=64)
-            scales = cod4.tile([P, KP], U8, name="w4s", tag="w4s", align_bytes=64)
+        def quant_w(i):
+            cd = cod4.tile([P, KP], U32, name="w4c", tag="w4c", align_bytes=64)
+            sc = cod4.tile([P, KP], U8, name="w4s", tag="w4s", align_bytes=64)
             nc.vector.quantize_mx(
-                out=codes[:].bitcast(FP8X4),
-                scales=scales[:],
-                in_=w4g[i][:].rearrange("p t m j -> p (t m j)"),
+                out=cd[:].bitcast(FP8X4), scales=sc[:], in_=grouped[i][:].rearrange("p t m j -> p (t m j)")
             )
+            codes[i] = (cd, sc)
+
+        grouped5 = {}
+
+        def group_w5(c, half):
+            g_ = grp.tile([P, HJ, 4], BF16, name="wg5", tag="g5", align_bytes=64)
+            regroup(nc, g_, raw5[c][:, :, half * HJ : (half + 1) * HJ], HJ, NV_W5)
+            grouped5[c, half] = g_
+
+        def quant_w5(c, half):
+            cols = slice(half * HJ, (half + 1) * HJ)
+            nc.vector.quantize_mx(
+                out=w5c[c][:, cols].bitcast(FP8X4),
+                scales=w5s[c][:, cols],
+                in_=grouped5[c, half][:].rearrange("p c t -> p (c t)"),
+            )
+
+        def layer1(i):
+            g = i % NG
+            cd, sc = codes[i]
             for t in range(4):
                 if g == 0:
-                    ps1[t] = psa.tile([P, B], F32, name="ps1", tag="a")
+                    ps1[i // NG, t] = psa.tile([P, B], F32, name="ps1", tag="a")
                 nc.tensor.matmul_mx(
-                    out=ps1[t][:],
-                    lhsT=codes[:, t * P : (t + 1) * P].bitcast(FP8X4),
-                    lhsT_scale=scales[:, t * P : (t + 1) * P],
+                    out=ps1[i // NG, t][:],
+                    lhsT=cd[:, t * P : (t + 1) * P].bitcast(FP8X4),
+                    lhsT_scale=sc[:, t * P : (t + 1) * P],
                     rhs=h3c[:, g, :].bitcast(FP8X4),
                     rhs_scale=h3s[:, g, :],
                     start=(g == 0),
                     stop=(g == NG - 1),
                 )
 
-        def stage_c(c2, on_vector):
+        def relu_h4(c2, on_vector):
             hp = h4pool.tile([P, 4, B], BF16, name="h4p", tag="h4p")
             for t in range(4):
                 col = bias[:, c2, t : t + 1]
                 if t in on_vector:
                     nc.vector.tensor_scalar(
-                        out=hp[:, t, :], in0=ps1[t][:], scalar1=col, scalar2=0.0, op0=ALU.add, op1=ALU.max
+                        out=hp[:, t, :], in0=ps1[c2, t][:], scalar1=col, scalar2=0.0, op0=ALU.add, op1=ALU.max
                     )
                 else:
-                    nc.scalar.activation(out=hp[:, t, :], in_=ps1[t][:], func=ACT.Relu, bias=col, scale=1.0)
+                    nc.scalar.activation(out=hp[:, t, :], in_=ps1[c2, t][:], func=ACT.Relu, bias=col, scale=1.0)
             h4p[c2] = hp
 
-        def stage_d(c2, nv):
+        def group_h4(c2, nv):
             hg = h4pool.tile([P, B, 4], BF16, name="h4g", tag="h4g", align_bytes=64)
             regroup(nc, hg, h4p[c2], B, nv)
             h4g[c2] = hg
 
-        def stage_e(c2):
+        def quant_h4(c2):
             nc.vector.quantize_mx(
                 out=h4c[c2][:].bitcast(FP8X4),
                 scales=h4s[c2][:],
                 in_=h4g[c2][:].rearrange("p b t -> p (b t)"),
             )
 
-        for i in range(4 * NG + 1):
-            if i < 4 * NG:
-                stage_a(i)
-                if i + LOOKAHEAD < 4 * NG:
-                    load_w4(i + LOOKAHEAD)
-                if i + LOOKAHEAD == 4 * NG - 1:
-                    load_tail()
-            if i >= 6 and i % 4 == 2:
-                stage_d(i // 4 - 1, B)
-            if i >= 1:
-                stage_b(i - 1)
-                if (i - 1) % 4 == 3:
-                    last = i == 4 * NG
-                    stage_c((i - 1) // 4, (1, 3) if last else ())
-            if i >= 7 and i % 4 == 3:
-                stage_e(i // 4 - 1)
+        acc = {}
 
-        w5c = keep.tile([P, NG, HALF], U32, name="w5c", align_bytes=64)
-        w5s = keep.tile([P, NG, HALF], U8, name="w5s", align_bytes=64)
-        w5g = {}
-
-        def stage_a5(c):
-            g_ = grp.tile([P, HALF, 4], BF16, name="wg5", tag="g", align_bytes=64)
-            regroup(nc, g_, w5r[c], HALF, NV_W)
-            w5g[c] = g_
-
-        def stage_q5(c):
-            nc.vector.quantize_mx(
-                out=w5c[:, c, :].bitcast(FP8X4),
-                scales=w5s[:, c, :],
-                in_=w5g[c][:].rearrange("p c t -> p (c t)"),
-            )
-
-        stage_a5(0)
-        stage_a5(1)
-        stage_d(3, 320)
-        stage_q5(0)
-        stage_a5(2)
-        stage_e(3)
-        stage_q5(1)
-        stage_a5(3)
-        stage_q5(2)
-        stage_q5(3)
-
-        acc = [psa.tile([P, B], F32, name="acc%d" % jt, tag="a") for jt in range(4)]
-        for c in range(NG):
-            for jt in range(4):
+        def layer2(c, half):
+            for jt in (2 * half, 2 * half + 1):
+                if c == 0:
+                    acc[jt] = psa.tile([P, B], F32, name="acc", tag="a")
                 nc.tensor.matmul_mx(
                     out=acc[jt][:],
-                    lhsT=w5c[:, c, jt * P : (jt + 1) * P].bitcast(FP8X4),
-                    lhsT_scale=w5s[:, c, jt * P : (jt + 1) * P],
+                    lhsT=w5c[c][:, jt * P : (jt + 1) * P].bitcast(FP8X4),
+                    lhsT_scale=w5s[c][:, jt * P : (jt + 1) * P],
                     rhs=h4c[c][:].bitcast(FP8X4),
                     rhs_scale=h4s[c][:],
                     start=(c == 0),
                     stop=(c == NG - 1),
                 )
 
-        zt = []
-        for jt in range(4):
+        zt = {}
+
+        def add_b5(jt):
             z = keep.tile([P, B], F32, name="zt%d" % jt)
             col = bias5[:, jt : jt + 1]
             if jt % 2 == 0:
                 nc.scalar.activation(out=z[:], in_=acc[jt][:], func=ACT.Identity, bias=col, scale=1.0)
             else:
                 nc.vector.tensor_scalar(out=z[:], in0=acc[jt][:], scalar1=col, scalar2=None, op0=ALU.add)
-            zt.append(z)
-        n_exit = 0
-        for ch in range(2):
-            for bt in range(NBT):
-                f = psa.tile([P, 2, 256], F32, name="f", tag="a")
+            zt[jt] = z
+
+        fin = {}
+
+        def add_x(bt, half):
+            f = psa.tile([P, 2, HJ], F32, name="f", tag="a")
+            nc.tensor.matmul(
+                out=f[:],
+                lhsT=identb[:],
+                rhs=xr[bt][:, half * HALF : (half + 1) * HALF].rearrange("p (j e) -> p e j", e=2),
+                start=True,
+                stop=False,
+            )
+            fin[bt, half] = f
+
+        def add_m(bt, half):
+            for r in range(2):
                 nc.tensor.matmul(
-                    out=f[:],
-                    lhsT=identb[:],
-                    rhs=xr[bt][:, ch * 512 : (ch + 1) * 512].rearrange("p (j e) -> p e j", e=2),
-                    start=True,
-                    stop=False,
+                    out=fin[bt, half][:, 0, r * P : (r + 1) * P],
+                    lhsT=zt[2 * half + r][:, bt * P : (bt + 1) * P],
+                    rhs=ident[:],
+                    is_transpose=True,
+                    start=False,
+                    stop=(r == 1),
                 )
-                for r in range(2):
-                    nc.tensor.matmul(
-                        out=f[:, 0, r * P : (r + 1) * P],
-                        lhsT=zt[2 * ch + r][:, bt * P : (bt + 1) * P],
-                        rhs=ident[:],
-                        is_transpose=True,
-                        start=False,
-                        stop=(r == 1),
-                    )
-                o = opool.tile([P, 256, 2], F32, name="o", tag="o")
-                if n_exit % 2 == 0:
-                    nc.scalar.copy(out=o[:], in_=f[:].rearrange("p e j -> p j e"))
-                else:
-                    nc.vector.tensor_copy(out=o[:], in_=f[:].rearrange("p e j -> p j e"))
-                n_exit += 1
-                nc.sync.dma_start(
-                    out=out[bt * P : (bt + 1) * P, ch * 512 : (ch + 1) * 512],
-                    in_=o[:].rearrange("p j e -> p (j e)"),
-                )
+
+        def store(bt, half):
+            o = opool.tile([P, HJ, 2], F32, name="o", tag="o")
+            src = fin[bt, half][:].rearrange("p e j -> p j e")
+            if bt % 2 == 0:
+                nc.scalar.copy(out=o[:], in_=src)
+            else:
+                nc.vector.tensor_copy(out=o[:], in_=src)
+            nc.sync.dma_start(
+                out=out[bt * P : (bt + 1) * P, half * HALF : (half + 1) * HALF],
+                in_=o[:].rearrange("p j e -> p (j e)"),
+            )
+
+        for i in range(HEAD):
+            group_w(i)
+        for i in range(HEAD):
+            quant_w(i)
+        for bt in range(NBT):
+            turn_h3(bt)
+        browf = const.tile([P, 512], F32, name="browf")
+        nc.vector.tensor_copy(out=browf[:], in_=brow[:])
+        quant_h3(0)
+        pb = psa.tile([P, 4, P], F32, name="pb", tag="a")
+        pb5 = psa.tile([P, 4, P], F32, name="pb5", tag="a")
+        for t in range(4):
+            nc.tensor.transpose(pb[:, t, :], browf[:, t : 512 : 4], ident[:])
+        for t in range(4):
+            nc.tensor.transpose(pb5[:, t, :], browf[:, t * P : (t + 1) * P], ident[:])
+        quant_h3(1)
+        group_w(HEAD)
+        quant_h3(2)
+        quant_h3(3)
+        bias = const.tile([P, 4, 4], F32, name="bias")
+        nc.vector.tensor_copy(out=bias[:], in_=pb[:, :, 0:4].rearrange("p t c -> p c t"))
+        bias5 = const.tile([P, 4], F32, name="bias5")
+        nc.vector.tensor_copy(out=bias5[:], in_=pb5[:, :, 4])
+        for i in range(HEAD):
+            layer1(i)
+
+        for i in range(HEAD, NCH):
+            if i + 1 < NCH:
+                group_w(i + 1)
+            else:
+                group_w5(0, 0)
+            quant_w(i)
+            layer1(i)
+            if i >= 4 and i % 4 == 0:
+                relu_h4(i // 4 - 1, ())
+            if i >= 5 and i % 4 == 1:
+                group_h4(i // 4 - 1, B)
+            if i >= 6 and i % 4 == 2:
+                quant_h4(i // 4 - 1)
+
+        group_w5(1, 0)
+        quant_w5(0, 0)
+        group_w5(2, 0)
+        quant_w5(1, 0)
+        relu_h4(3, (1, 3))
+        group_w5(3, 0)
+        quant_w5(2, 0)
+        for c in range(3):
+            layer2(c, 0)
+        group_h4(3, 320)
+        quant_w5(3, 0)
+        for bt in range(NBT):
+            add_x(bt, 0)
+        quant_h4(3)
+        layer2(3, 0)
+
+        group_w5(0, 1)
+        add_b5(0)
+        group_w5(1, 1)
+        add_b5(1)
+        quant_w5(0, 1)
+        for bt in range(NBT):
+            add_m(bt, 0)
+        group_w5(2, 1)
+        store(0, 0)
+        store(1, 0)
+        quant_w5(1, 1)
+        group_w5(3, 1)
+        for c in range(2):
+            layer2(c, 1)
+        quant_w5(2, 1)
+        quant_w5(3, 1)
+        store(2, 0)
+        store(3, 0)
+        for c in range(2, 4):
+            layer2(c, 1)
+        for bt in range(NBT):
+            add_x(bt, 1)
+        add_b5(2)
+        add_b5(3)
+        for bt in range(NBT):
+            add_m(bt, 1)
+            store(bt, 1)

@@ -42,11 +42,11 @@ def regroup(nc, dst, src, width, nv):
 
 
 def regroup_w4(nc, dst, src, nv):
-    d = dst[:].rearrange("p t (a b) j -> p t a j b", b=MH)
-    s = src[:].rearrange("p j (a b t) -> p t a j b", b=MH, t=4)
+    d = dst[:].rearrange("p t (a b) j -> p a j t b", b=MH)
+    s = src[:].rearrange("p j (a b t) -> p a j t b", b=MH, t=4)
     cut = nv // (4 * MH)
-    nc.vector.tensor_copy(out=d[:, :, 0:cut], in_=s[:, :, 0:cut])
-    nc.scalar.copy(out=d[:, :, cut:], in_=s[:, :, cut:])
+    nc.vector.tensor_copy(out=d[:, 0:cut], in_=s[:, 0:cut])
+    nc.scalar.copy(out=d[:, cut:], in_=s[:, cut:])
 
 
 def tile_additivecoupling_pa_kernel(tc, x, h3, W4, b4, W5, b5, out):

@@ -21,32 +21,35 @@ NBT = B // P
 
 FLOPS = 2 * B * MID * MID + 2 * B * MID * HALF
 
-HEAD = 2
 NCH = 16
-HJ = HALF // 2
-NV_W5 = HJ // 2
-NV_W = 240
+NV_W5 = P // 2
 MH = 2
 
 
-def regroup(nc, dst, src, width, nv):
-    nc.vector.tensor_copy(
-        out=dst[:, 0:nv, :].rearrange("p (c i) t -> p c t i", i=4),
-        in_=src[:, :, 0:nv].rearrange("p t (c i) -> p c t i", i=4),
-    )
-    if nv < width:
-        nc.scalar.copy(
-            out=dst[:, nv:width, :].rearrange("p (c i) t -> p c t i", i=4),
-            in_=src[:, :, nv:width].rearrange("p t (c i) -> p c t i", i=4),
-        )
-
-
-def regroup_w4(nc, dst, src, nv):
-    d = dst[:].rearrange("p t (a b) j -> p a j t b", b=MH)
-    s = src[:].rearrange("p j (a b t) -> p a j t b", b=MH, t=4)
-    cut = nv // (4 * MH)
+def regroup_h4(nc, dst, src, nv):
+    d = dst[:].rearrange("p (a i) t -> p a t i", i=4)
+    s = src[:].rearrange("p t (a i) -> p a t i", i=4)
+    cut = nv // 4
     nc.vector.tensor_copy(out=d[:, 0:cut], in_=s[:, 0:cut])
-    nc.scalar.copy(out=d[:, cut:], in_=s[:, cut:])
+    if nv < B:
+        nc.scalar.copy(out=d[:, cut:], in_=s[:, cut:])
+
+
+def regroup_w5(nc, dst, src, nv):
+    d = dst[:].rearrange("p c (a i) t -> p c a t i", i=4)
+    s = src.rearrange("p c t (a i) -> p c a t i", i=4)
+    cut = nv // 4
+    if nv > 0:
+        nc.vector.tensor_copy(out=d[:, :, 0:cut], in_=s[:, :, 0:cut])
+    if nv < P:
+        nc.scalar.copy(out=d[:, :, cut:], in_=s[:, :, cut:])
+
+
+def regroup_w4(copy, dst, src):
+    copy(
+        out=dst.rearrange("p t (a b) j -> p a j t b", b=MH),
+        in_=src[:].rearrange("p j (a b t) -> p a j t b", b=MH, t=4),
+    )
 
 
 def tile_additivecoupling_pa_kernel(tc, x, h3, W4, b4, W5, b5, out):
@@ -54,9 +57,9 @@ def tile_additivecoupling_pa_kernel(tc, x, h3, W4, b4, W5, b5, out):
     with ExitStack() as ctx:
         const = ctx.enter_context(tc.tile_pool(name="const", bufs=1))
         keep = ctx.enter_context(tc.tile_pool(name="keep", bufs=1))
-        raw4 = ctx.enter_context(tc.tile_pool(name="raw4", bufs=NCH))
-        grp = ctx.enter_context(tc.tile_pool(name="grp", bufs=4))
-        cod4 = ctx.enter_context(tc.tile_pool(name="cod4", bufs=6))
+        raw4 = ctx.enter_context(tc.tile_pool(name="raw4", bufs=10))
+        grp = ctx.enter_context(tc.tile_pool(name="grp", bufs=3))
+        cod4 = ctx.enter_context(tc.tile_pool(name="cod4", bufs=4))
         h4pool = ctx.enter_context(tc.tile_pool(name="h4pool", bufs=2))
         opool = ctx.enter_context(tc.tile_pool(name="opool", bufs=8))
         psa = ctx.enter_context(tc.psum_pool(name="psa", bufs=8))
@@ -70,7 +73,6 @@ def tile_additivecoupling_pa_kernel(tc, x, h3, W4, b4, W5, b5, out):
         nc.vector.tensor_copy(out=identb[:], in_=ident[:])
 
         raw = []
-        raw5 = []
 
         def load_w4(i):
             c2, g = divmod(i, NG)
@@ -81,7 +83,7 @@ def tile_additivecoupling_pa_kernel(tc, x, h3, W4, b4, W5, b5, out):
             )
             raw.append(r)
 
-        for i in range(HEAD):
+        for i in range(2):
             load_w4(i)
         h3r = []
         for bt in range(NBT):
@@ -90,14 +92,13 @@ def tile_additivecoupling_pa_kernel(tc, x, h3, W4, b4, W5, b5, out):
             h3r.append(t_)
         nc.sync.dma_start(out=brow[0:4, :], in_=b4.rearrange("(r c) -> r c", c=512))
         nc.sync.dma_start(out=brow[4:5, :], in_=b5.rearrange("(r c) -> r c", c=512))
-        for i in range(HEAD, NCH):
+        for i in range(2, NCH):
             load_w4(i)
+        raw5 = keep.tile([P, NG, 4, HALF], BF16, name="raw5")
         for c in range(NG):
-            r = keep.tile([P, 4, HALF], BF16, name="w5r%d" % c)
             nc.sync.dma_start(
-                out=r[:], in_=W5[c * KP : (c + 1) * KP, :].rearrange("(p t) j -> p t j", t=4)
+                out=raw5[:, c], in_=W5[c * KP : (c + 1) * KP, :].rearrange("(p t) j -> p t j", t=4)
             )
-            raw5.append(r)
         xr = []
         for bt in range(NBT):
             t_ = keep.tile([P, 2 * HALF], BF16, name="xr%d" % bt)
@@ -133,72 +134,73 @@ def tile_additivecoupling_pa_kernel(tc, x, h3, W4, b4, W5, b5, out):
         grouped = {}
         codes = {}
         ps1 = {}
-        h4p = {}
         h4g = {}
         h4c = [keep.tile([P, B], U32, name="h4c%d" % c, align_bytes=64) for c in range(NG)]
         h4s = [keep.tile([P, B], U8, name="h4s%d" % c, align_bytes=64) for c in range(NG)]
-        w5c = [keep.tile([P, HALF], U32, name="w5c%d" % c, align_bytes=64) for c in range(NG)]
-        w5s = [keep.tile([P, HALF], U8, name="w5s%d" % c, align_bytes=64) for c in range(NG)]
+        w5c = [keep.tile([P, NG, P], U32, name="w5c%d" % jt, align_bytes=64) for jt in range(4)]
+        w5s = [keep.tile([P, NG, P], U8, name="w5s%d" % jt, align_bytes=64) for jt in range(4)]
 
-        def group_w(i):
-            g_ = grp.tile([P, 4, P, 4], BF16, name="wg", tag="g", align_bytes=64)
-            regroup_w4(nc, g_, raw[i], NV_W)
-            grouped[i] = g_
+        def group_pair(q):
+            g_ = grp.tile([P, 2, 4, P, 4], BF16, name="wg", tag="g", align_bytes=64)
+            regroup_w4(nc.vector.tensor_copy, g_[:, 0], raw[2 * q])
+            regroup_w4(nc.scalar.copy, g_[:, 1], raw[2 * q + 1])
+            grouped[q] = g_
 
-        def quant_w(i):
-            cd = cod4.tile([P, KP], U32, name="w4c", tag="w4c", align_bytes=64)
-            sc = cod4.tile([P, KP], U8, name="w4s", tag="w4s", align_bytes=64)
+        def quant_pair(q):
+            cd = cod4.tile([P, 2, KP], U32, name="w4c", tag="w4c", align_bytes=64)
+            sc = cod4.tile([P, 2, KP], U8, name="w4s", tag="w4s", align_bytes=64)
             nc.vector.quantize_mx(
-                out=cd[:].bitcast(FP8X4), scales=sc[:], in_=grouped[i][:].rearrange("p t m j -> p (t m j)")
+                out=cd[:].rearrange("p u c -> p (u c)").bitcast(FP8X4),
+                scales=sc[:].rearrange("p u c -> p (u c)"),
+                in_=grouped[q][:].rearrange("p u t m j -> p (u t m j)"),
             )
-            codes[i] = (cd, sc)
+            codes[q] = (cd, sc)
 
         grouped5 = {}
 
-        def group_w5(c, half):
-            g_ = grp.tile([P, HJ, 4], BF16, name="wg5", tag="g5", align_bytes=64)
-            regroup(nc, g_, raw5[c][:, :, half * HJ : (half + 1) * HJ], HJ, NV_W5)
-            grouped5[c, half] = g_
+        def group_w5(jt):
+            g_ = grp.tile([P, NG, P, 4], BF16, name="wg5", tag="g5", align_bytes=64)
+            regroup_w5(nc, g_, raw5[:, :, :, jt * P : (jt + 1) * P], (P, 0, NV_W5, NV_W5)[jt])
+            grouped5[jt] = g_
 
-        def quant_w5(c, half):
-            cols = slice(half * HJ, (half + 1) * HJ)
+        def quant_w5(jt):
             nc.vector.quantize_mx(
-                out=w5c[c][:, cols].bitcast(FP8X4),
-                scales=w5s[c][:, cols],
-                in_=grouped5[c, half][:].rearrange("p c t -> p (c t)"),
+                out=w5c[jt][:].rearrange("p c j -> p (c j)").bitcast(FP8X4),
+                scales=w5s[jt][:].rearrange("p c j -> p (c j)"),
+                in_=grouped5[jt][:].rearrange("p c j t -> p (c j t)"),
             )
 
         def layer1(i):
-            g = i % NG
-            cd, sc = codes[i]
+            g, u = i % NG, i % 2
+            cd, sc = codes[i // 2]
             for t in range(4):
                 if g == 0:
                     ps1[i // NG, t] = psa.tile([P, B], F32, name="ps1", tag="a")
                 nc.tensor.matmul_mx(
                     out=ps1[i // NG, t][:],
-                    lhsT=cd[:, t * P : (t + 1) * P].bitcast(FP8X4),
-                    lhsT_scale=sc[:, t * P : (t + 1) * P],
+                    lhsT=cd[:, u, t * P : (t + 1) * P].bitcast(FP8X4),
+                    lhsT_scale=sc[:, u, t * P : (t + 1) * P],
                     rhs=h3c[:, g, :].bitcast(FP8X4),
                     rhs_scale=h3s[:, g, :],
                     start=(g == 0),
                     stop=(g == NG - 1),
                 )
 
-        def relu_h4(c2, on_vector):
-            hp = h4pool.tile([P, 4, B], BF16, name="h4p", tag="h4p")
-            for t in range(4):
-                col = bias[:, c2, t : t + 1]
-                if t in on_vector:
-                    nc.vector.tensor_scalar(
-                        out=hp[:, t, :], in0=ps1[c2, t][:], scalar1=col, scalar2=0.0, op0=ALU.add, op1=ALU.max
-                    )
+        h4p = {}
+
+        def relu_h4(c2, ts, engine):
+            if c2 not in h4p:
+                h4p[c2] = h4pool.tile([P, 4, B], BF16, name="h4p", tag="h4p")
+            for t in ts:
+                dst, src, col = h4p[c2][:, t, :], ps1[c2, t][:], bias[:, c2, t : t + 1]
+                if engine == "vector":
+                    nc.vector.tensor_scalar(out=dst, in0=src, scalar1=col, scalar2=0.0, op0=ALU.add, op1=ALU.max)
                 else:
-                    nc.scalar.activation(out=hp[:, t, :], in_=ps1[c2, t][:], func=ACT.Relu, bias=col, scale=1.0)
-            h4p[c2] = hp
+                    nc.scalar.activation(out=dst, in_=src, func=ACT.Relu, bias=col, scale=1.0)
 
         def group_h4(c2, nv):
             hg = h4pool.tile([P, B, 4], BF16, name="h4g", tag="h4g", align_bytes=64)
-            regroup(nc, hg, h4p[c2], B, nv)
+            regroup_h4(nc, hg, h4p[c2], nv)
             h4g[c2] = hg
 
         def quant_h4(c2):
@@ -210,14 +212,14 @@ def tile_additivecoupling_pa_kernel(tc, x, h3, W4, b4, W5, b5, out):
 
         acc = {}
 
-        def layer2(c, half):
-            for jt in (2 * half, 2 * half + 1):
+        def layer2(jt, cs):
+            for c in cs:
                 if c == 0:
                     acc[jt] = psa.tile([P, B], F32, name="acc", tag="a")
                 nc.tensor.matmul_mx(
                     out=acc[jt][:],
-                    lhsT=w5c[c][:, jt * P : (jt + 1) * P].bitcast(FP8X4),
-                    lhsT_scale=w5s[c][:, jt * P : (jt + 1) * P],
+                    lhsT=w5c[jt][:, c, :].bitcast(FP8X4),
+                    lhsT_scale=w5s[jt][:, c, :],
                     rhs=h4c[c][:].bitcast(FP8X4),
                     rhs_scale=h4s[c][:],
                     start=(c == 0),
@@ -237,48 +239,51 @@ def tile_additivecoupling_pa_kernel(tc, x, h3, W4, b4, W5, b5, out):
 
         fin = {}
 
-        def add_x(bt, half):
-            f = psa.tile([P, 2, HJ], F32, name="f", tag="a")
-            nc.tensor.matmul(
-                out=f[:],
-                lhsT=identb[:],
-                rhs=xr[bt][:, half * HALF : (half + 1) * HALF].rearrange("p (j e) -> p e j", e=2),
-                start=True,
-                stop=False,
-            )
-            fin[bt, half] = f
+        def add_x_m(jt):
+            for pr in range(2):
+                f = psa.tile([P, 2, 2, P], F32, name="f", tag="a")
+                for b in range(2):
+                    bt = 2 * pr + b
+                    nc.tensor.matmul(
+                        out=f[:, b],
+                        lhsT=identb[:],
+                        rhs=xr[bt][:, jt * 2 * P : (jt + 1) * 2 * P].rearrange("p (j e) -> p e j", e=2),
+                        start=True,
+                        stop=False,
+                    )
+                    nc.tensor.matmul(
+                        out=f[:, b, 0, :],
+                        lhsT=zt[jt][:, bt * P : (bt + 1) * P],
+                        rhs=ident[:],
+                        is_transpose=True,
+                        start=False,
+                        stop=True,
+                    )
+                fin[jt, pr] = f
 
-        def add_m(bt, half):
-            for r in range(2):
-                nc.tensor.matmul(
-                    out=fin[bt, half][:, 0, r * P : (r + 1) * P],
-                    lhsT=zt[2 * half + r][:, bt * P : (bt + 1) * P],
-                    rhs=ident[:],
-                    is_transpose=True,
-                    start=False,
-                    stop=(r == 1),
+        def store(jt):
+            for pr in range(2):
+                o = opool.tile([P, 2, P, 2], F32, name="o", tag="o")
+                src = fin[jt, pr][:].rearrange("p b e j -> p b j e")
+                if pr == 0:
+                    nc.scalar.copy(out=o[:], in_=src)
+                else:
+                    nc.vector.tensor_copy(out=o[:], in_=src)
+                nc.sync.dma_start(
+                    out=out[2 * pr * P : (2 * pr + 2) * P, jt * 2 * P : (jt + 1) * 2 * P].rearrange(
+                        "(b p) c -> p b c", p=P
+                    ),
+                    in_=o[:].rearrange("p b j e -> p b (j e)"),
                 )
 
-        def store(bt, half):
-            o = opool.tile([P, HJ, 2], F32, name="o", tag="o")
-            src = fin[bt, half][:].rearrange("p e j -> p j e")
-            if bt % 2 == 0:
-                nc.scalar.copy(out=o[:], in_=src)
-            else:
-                nc.vector.tensor_copy(out=o[:], in_=src)
-            nc.sync.dma_start(
-                out=out[bt * P : (bt + 1) * P, half * HALF : (half + 1) * HALF],
-                in_=o[:].rearrange("p j e -> p (j e)"),
-            )
-
-        for i in range(HEAD):
-            group_w(i)
-        for i in range(HEAD):
-            quant_w(i)
-        for bt in range(NBT):
+        group_pair(0)
+        turn_h3(0)
+        quant_pair(0)
+        for bt in range(1, NBT):
             turn_h3(bt)
         browf = const.tile([P, 512], F32, name="browf")
         nc.vector.tensor_copy(out=browf[:], in_=brow[:])
+        group_pair(1)
         quant_h3(0)
         pb = psa.tile([P, 4, P], F32, name="pb", tag="a")
         pb5 = psa.tile([P, 4, P], F32, name="pb5", tag="a")
@@ -287,70 +292,57 @@ def tile_additivecoupling_pa_kernel(tc, x, h3, W4, b4, W5, b5, out):
         for t in range(4):
             nc.tensor.transpose(pb5[:, t, :], browf[:, t * P : (t + 1) * P], ident[:])
         quant_h3(1)
-        group_w(HEAD)
         quant_h3(2)
         quant_h3(3)
         bias = const.tile([P, 4, 4], F32, name="bias")
         nc.vector.tensor_copy(out=bias[:], in_=pb[:, :, 0:4].rearrange("p t c -> p c t"))
         bias5 = const.tile([P, 4], F32, name="bias5")
         nc.vector.tensor_copy(out=bias5[:], in_=pb5[:, :, 4])
-        for i in range(HEAD):
+        for i in range(2):
             layer1(i)
 
-        for i in range(HEAD, NCH):
-            if i + 1 < NCH:
-                group_w(i + 1)
+        for q in range(1, NCH // 2):
+            if q + 1 < NCH // 2:
+                group_pair(q + 1)
             else:
-                group_w5(0, 0)
-            quant_w(i)
-            layer1(i)
-            if i >= 4 and i % 4 == 0:
-                relu_h4(i // 4 - 1, ())
-            if i >= 5 and i % 4 == 1:
-                group_h4(i // 4 - 1, B)
-            if i >= 6 and i % 4 == 2:
-                quant_h4(i // 4 - 1)
+                group_w5(0)
+            quant_pair(q)
+            layer1(2 * q)
+            layer1(2 * q + 1)
+            if q >= 3 and q % 2 == 1:
+                relu_h4((q - 3) // 2, range(4), "scalar")
+            if q >= 4 and q % 2 == 0:
+                group_h4((q - 4) // 2, B)
+            if q >= 5 and q % 2 == 1:
+                quant_h4((q - 5) // 2)
 
-        group_w5(1, 0)
-        quant_w5(0, 0)
-        group_w5(2, 0)
-        quant_w5(1, 0)
-        relu_h4(3, (1, 3))
-        group_w5(3, 0)
-        quant_w5(2, 0)
-        for c in range(3):
-            layer2(c, 0)
+        group_w5(1)
+        quant_w5(0)
+        group_h4(2, B)
+        group_w5(2)
+        quant_h4(2)
+        quant_w5(1)
+        relu_h4(3, range(4), "scalar")
+        layer2(0, (0, 1, 2))
+        layer2(1, (0, 1, 2))
+        quant_w5(2)
         group_h4(3, 320)
-        quant_w5(3, 0)
-        for bt in range(NBT):
-            add_x(bt, 0)
         quant_h4(3)
-        layer2(3, 0)
-
-        group_w5(0, 1)
+        layer2(0, (3,))
+        layer2(1, (3,))
+        layer2(2, (0, 1, 2, 3))
         add_b5(0)
-        group_w5(1, 1)
+        group_w5(3)
         add_b5(1)
-        quant_w5(0, 1)
-        for bt in range(NBT):
-            add_m(bt, 0)
-        group_w5(2, 1)
-        store(0, 0)
-        store(1, 0)
-        quant_w5(1, 1)
-        group_w5(3, 1)
-        for c in range(2):
-            layer2(c, 1)
-        quant_w5(2, 1)
-        quant_w5(3, 1)
-        store(2, 0)
-        store(3, 0)
-        for c in range(2, 4):
-            layer2(c, 1)
-        for bt in range(NBT):
-            add_x(bt, 1)
+        add_x_m(0)
+        add_x_m(1)
+        quant_w5(3)
+        layer2(3, (0, 1, 2, 3))
+        store(0)
         add_b5(2)
+        add_x_m(2)
+        store(1)
         add_b5(3)
-        for bt in range(NBT):
-            add_m(bt, 1)
-            store(bt, 1)
+        add_x_m(3)
+        store(2)
+        store(3)

@@ -22,7 +22,9 @@ NBT = B // P
 FLOPS = 2 * B * MID * MID + 2 * B * MID * HALF
 
 NCH = 16
-NV_W5 = P // 2
+PAIRS = [(g, NG + g) for g in range(NG)] + [(i, i + 1) for i in range(2 * NG, NCH, 2)]
+RELU_STEP = {4: 0, 5: 1, 7: 2}
+NV_W5 = (P, 0, 64, 32)
 MH = 2
 
 
@@ -48,7 +50,7 @@ def regroup_w5(nc, dst, src, nv):
 def regroup_w4(copy, dst, src):
     copy(
         out=dst.rearrange("p t (a b) j -> p a j t b", b=MH),
-        in_=src[:].rearrange("p j (a b t) -> p a j t b", b=MH, t=4),
+        in_=src.rearrange("p j (a b t) -> p a j t b", b=MH, t=4),
     )
 
 
@@ -57,7 +59,8 @@ def tile_additivecoupling_pa_kernel(tc, x, h3, W4, b4, W5, b5, out):
     with ExitStack() as ctx:
         const = ctx.enter_context(tc.tile_pool(name="const", bufs=1))
         keep = ctx.enter_context(tc.tile_pool(name="keep", bufs=1))
-        raw4 = ctx.enter_context(tc.tile_pool(name="raw4", bufs=10))
+        raw8 = ctx.enter_context(tc.tile_pool(name="raw8", bufs=3))
+        raw4 = ctx.enter_context(tc.tile_pool(name="raw4", bufs=6))
         grp = ctx.enter_context(tc.tile_pool(name="grp", bufs=3))
         cod4 = ctx.enter_context(tc.tile_pool(name="cod4", bufs=4))
         h4pool = ctx.enter_context(tc.tile_pool(name="h4pool", bufs=2))
@@ -72,7 +75,15 @@ def tile_additivecoupling_pa_kernel(tc, x, h3, W4, b4, W5, b5, out):
         identb = const.tile([P, P], BF16, name="identb")
         nc.vector.tensor_copy(out=identb[:], in_=ident[:])
 
-        raw = []
+        raw = {}
+
+        def load_w4_pair(g):
+            r = raw8.tile([P, 4, 2 * KP], BF16, name="w4d", tag="w4d")
+            nc.sync.dma_start(
+                out=r[:], in_=W4[g * KP : (g + 1) * KP, 0 : 2 * KP].rearrange("(p j) c -> p j c", j=4)
+            )
+            raw[g] = r[:, :, 0:KP]
+            raw[NG + g] = r[:, :, KP : 2 * KP]
 
         def load_w4(i):
             c2, g = divmod(i, NG)
@@ -81,9 +92,9 @@ def tile_additivecoupling_pa_kernel(tc, x, h3, W4, b4, W5, b5, out):
                 out=r[:],
                 in_=W4[g * KP : (g + 1) * KP, c2 * KP : (c2 + 1) * KP].rearrange("(p j) c -> p j c", j=4),
             )
-            raw.append(r)
+            raw[i] = r[:]
 
-        for i in range(2):
+        for i in PAIRS[0]:
             load_w4(i)
         h3r = []
         for bt in range(NBT):
@@ -92,7 +103,9 @@ def tile_additivecoupling_pa_kernel(tc, x, h3, W4, b4, W5, b5, out):
             h3r.append(t_)
         nc.sync.dma_start(out=brow[0:4, :], in_=b4.rearrange("(r c) -> r c", c=512))
         nc.sync.dma_start(out=brow[4:5, :], in_=b5.rearrange("(r c) -> r c", c=512))
-        for i in range(2, NCH):
+        for g in range(1, NG):
+            load_w4_pair(g)
+        for i in range(2 * NG, NCH):
             load_w4(i)
         raw5 = keep.tile([P, NG, 4, HALF], BF16, name="raw5")
         for c in range(NG):
@@ -142,8 +155,8 @@ def tile_additivecoupling_pa_kernel(tc, x, h3, W4, b4, W5, b5, out):
 
         def group_pair(q):
             g_ = grp.tile([P, 2, 4, P, 4], BF16, name="wg", tag="g", align_bytes=64)
-            regroup_w4(nc.vector.tensor_copy, g_[:, 0], raw[2 * q])
-            regroup_w4(nc.scalar.copy, g_[:, 1], raw[2 * q + 1])
+            regroup_w4(nc.vector.tensor_copy, g_[:, 0], raw[PAIRS[q][0]])
+            regroup_w4(nc.scalar.copy, g_[:, 1], raw[PAIRS[q][1]])
             grouped[q] = g_
 
         def quant_pair(q):
@@ -154,13 +167,14 @@ def tile_additivecoupling_pa_kernel(tc, x, h3, W4, b4, W5, b5, out):
                 scales=sc[:].rearrange("p u c -> p (u c)"),
                 in_=grouped[q][:].rearrange("p u t m j -> p (u t m j)"),
             )
-            codes[q] = (cd, sc)
+            for u in range(2):
+                codes[PAIRS[q][u]] = cd[:, u, :], sc[:, u, :]
 
         grouped5 = {}
 
         def group_w5(jt):
             g_ = grp.tile([P, NG, P, 4], BF16, name="wg5", tag="g5", align_bytes=64)
-            regroup_w5(nc, g_, raw5[:, :, :, jt * P : (jt + 1) * P], (P, 0, NV_W5, NV_W5)[jt])
+            regroup_w5(nc, g_, raw5[:, :, :, jt * P : (jt + 1) * P], NV_W5[jt])
             grouped5[jt] = g_
 
         def quant_w5(jt):
@@ -171,15 +185,15 @@ def tile_additivecoupling_pa_kernel(tc, x, h3, W4, b4, W5, b5, out):
             )
 
         def layer1(i):
-            g, u = i % NG, i % 2
-            cd, sc = codes[i // 2]
+            g = i % NG
+            cd, sc = codes[i]
             for t in range(4):
                 if g == 0:
                     ps1[i // NG, t] = psa.tile([P, B], F32, name="ps1", tag="a")
                 nc.tensor.matmul_mx(
                     out=ps1[i // NG, t][:],
-                    lhsT=cd[:, u, t * P : (t + 1) * P].bitcast(FP8X4),
-                    lhsT_scale=sc[:, u, t * P : (t + 1) * P],
+                    lhsT=cd[:, t * P : (t + 1) * P].bitcast(FP8X4),
+                    lhsT_scale=sc[:, t * P : (t + 1) * P],
                     rhs=h3c[:, g, :].bitcast(FP8X4),
                     rhs_scale=h3s[:, g, :],
                     start=(g == 0),
@@ -239,42 +253,39 @@ def tile_additivecoupling_pa_kernel(tc, x, h3, W4, b4, W5, b5, out):
 
         fin = {}
 
-        def add_x_m(jt):
-            for pr in range(2):
-                f = psa.tile([P, 2, 2, P], F32, name="f", tag="a")
-                for b in range(2):
-                    bt = 2 * pr + b
-                    nc.tensor.matmul(
-                        out=f[:, b],
-                        lhsT=identb[:],
-                        rhs=xr[bt][:, jt * 2 * P : (jt + 1) * 2 * P].rearrange("p (j e) -> p e j", e=2),
-                        start=True,
-                        stop=False,
-                    )
-                    nc.tensor.matmul(
-                        out=f[:, b, 0, :],
-                        lhsT=zt[jt][:, bt * P : (bt + 1) * P],
-                        rhs=ident[:],
-                        is_transpose=True,
-                        start=False,
-                        stop=True,
-                    )
-                fin[jt, pr] = f
+        def add_x(bt, half):
+            f = psa.tile([P, 2, 2 * P], F32, name="f", tag="a")
+            nc.tensor.matmul(
+                out=f[:],
+                lhsT=identb[:],
+                rhs=xr[bt][:, half * HALF : (half + 1) * HALF].rearrange("p (j e) -> p e j", e=2),
+                start=True,
+                stop=False,
+            )
+            fin[bt, half] = f
 
-        def store(jt):
-            for pr in range(2):
-                o = opool.tile([P, 2, P, 2], F32, name="o", tag="o")
-                src = fin[jt, pr][:].rearrange("p b e j -> p b j e")
-                if pr == 0:
-                    nc.scalar.copy(out=o[:], in_=src)
-                else:
-                    nc.vector.tensor_copy(out=o[:], in_=src)
-                nc.sync.dma_start(
-                    out=out[2 * pr * P : (2 * pr + 2) * P, jt * 2 * P : (jt + 1) * 2 * P].rearrange(
-                        "(b p) c -> p b c", p=P
-                    ),
-                    in_=o[:].rearrange("p b j e -> p b (j e)"),
+        def add_m(bt, half):
+            for r in range(2):
+                nc.tensor.matmul(
+                    out=fin[bt, half][:, 0, r * P : (r + 1) * P],
+                    lhsT=zt[2 * half + r][:, bt * P : (bt + 1) * P],
+                    rhs=ident[:],
+                    is_transpose=True,
+                    start=False,
+                    stop=(r == 1),
                 )
+
+        def store(bt, half):
+            o = opool.tile([P, 2 * P, 2], F32, name="o", tag="o")
+            src = fin[bt, half][:].rearrange("p e j -> p j e")
+            if bt % 2 == 0:
+                nc.scalar.copy(out=o[:], in_=src)
+            else:
+                nc.vector.tensor_copy(out=o[:], in_=src)
+            nc.sync.dma_start(
+                out=out[bt * P : (bt + 1) * P, half * HALF : (half + 1) * HALF],
+                in_=o[:].rearrange("p j e -> p (j e)"),
+            )
 
         group_pair(0)
         turn_h3(0)
@@ -298,23 +309,23 @@ def tile_additivecoupling_pa_kernel(tc, x, h3, W4, b4, W5, b5, out):
         nc.vector.tensor_copy(out=bias[:], in_=pb[:, :, 0:4].rearrange("p t c -> p c t"))
         bias5 = const.tile([P, 4], F32, name="bias5")
         nc.vector.tensor_copy(out=bias5[:], in_=pb5[:, :, 4])
-        for i in range(2):
+        for i in PAIRS[0]:
             layer1(i)
 
-        for q in range(1, NCH // 2):
-            if q + 1 < NCH // 2:
+        for q in range(1, len(PAIRS)):
+            if q + 1 < len(PAIRS):
                 group_pair(q + 1)
             else:
                 group_w5(0)
+            if q in RELU_STEP:
+                relu_h4(RELU_STEP[q], range(4), "scalar")
             quant_pair(q)
-            layer1(2 * q)
-            layer1(2 * q + 1)
-            if q >= 3 and q % 2 == 1:
-                relu_h4((q - 3) // 2, range(4), "scalar")
-            if q >= 4 and q % 2 == 0:
-                group_h4((q - 4) // 2, B)
-            if q >= 5 and q % 2 == 1:
-                quant_h4((q - 5) // 2)
+            for i in PAIRS[q]:
+                layer1(i)
+            if q - 1 in RELU_STEP:
+                group_h4(RELU_STEP[q - 1], B)
+            if q - 2 in RELU_STEP:
+                quant_h4(RELU_STEP[q - 2])
 
         group_w5(1)
         quant_w5(0)
@@ -327,22 +338,28 @@ def tile_additivecoupling_pa_kernel(tc, x, h3, W4, b4, W5, b5, out):
         layer2(1, (0, 1, 2))
         quant_w5(2)
         group_h4(3, 320)
+        for bt in range(NBT):
+            add_x(bt, 0)
         quant_h4(3)
         layer2(0, (3,))
         layer2(1, (3,))
         layer2(2, (0, 1, 2, 3))
-        add_b5(0)
         group_w5(3)
+        add_b5(0)
         add_b5(1)
-        add_x_m(0)
-        add_x_m(1)
+        for bt in range(NBT):
+            add_m(bt, 0)
         quant_w5(3)
         layer2(3, (0, 1, 2, 3))
-        store(0)
+        store(0, 0)
+        store(1, 0)
         add_b5(2)
-        add_x_m(2)
-        store(1)
+        store(2, 0)
+        store(3, 0)
+        for bt in range(NBT):
+            add_x(bt, 1)
         add_b5(3)
-        add_x_m(3)
-        store(2)
-        store(3)
+        for bt in range(NBT):
+            add_m(bt, 1)
+        for bt in range(NBT):
+            store(bt, 1)

@@ -94,7 +94,7 @@ def tile_additivecoupling_pa_kernel(tc, x, h3, W4, b4, W5, b5, out):
             )
             raw[i] = r[:]
 
-        for i in PAIRS[0]:
+        for i in reversed(PAIRS[0]):
             load_w4(i)
         h3r = []
         for bt in range(NBT):
@@ -105,8 +105,9 @@ def tile_additivecoupling_pa_kernel(tc, x, h3, W4, b4, W5, b5, out):
         nc.sync.dma_start(out=brow[4:5, :], in_=b5.rearrange("(r c) -> r c", c=512))
         for g in range(1, NG):
             load_w4_pair(g)
-        for i in range(2 * NG, NCH):
-            load_w4(i)
+        for q in range(NG, len(PAIRS)):
+            for i in reversed(PAIRS[q]):
+                load_w4(i)
         raw5 = keep.tile([P, NG, 4, HALF], BF16, name="raw5")
         for c in range(NG):
             nc.sync.dma_start(

from contextlib import ExitStack

import concourse.mybir as mybir
from concourse.masks import make_identity

F32 = mybir.dt.float32
BF16 = mybir.dt.bfloat16
U32 = mybir.dt.uint32
U8 = mybir.dt.uint8
FP8X4 = mybir.dt.float8_e4m3fn_x4
ACT = mybir.ActivationFunctionType
ALU = mybir.AluOpType

P = 128
B = 512
MID = 2048
HALF = 512
KP = 512
NG = MID // KP
NBT = B // P

FLOPS = 2 * B * MID * MID + 2 * B * MID * HALF

NCH = 16
PAIRS = [(g, NG + g) for g in range(NG)] + [(i, i + 1) for i in range(2 * NG, NCH, 2)]
RELU_STEP = {4: 0, 5: 1, 7: 2}
NV_W5 = (P, 0, 64, 32)
MH = 2


def regroup_h4(nc, dst, src, nv):
    d = dst[:].rearrange("p (a i) t -> p a t i", i=4)
    s = src[:].rearrange("p t (a i) -> p a t i", i=4)
    cut = nv // 4
    nc.vector.tensor_copy(out=d[:, 0:cut], in_=s[:, 0:cut])
    if nv < B:
        nc.scalar.copy(out=d[:, cut:], in_=s[:, cut:])


def regroup_w5(nc, dst, src, nv):
    d = dst[:].rearrange("p c (a i) t -> p c a t i", i=4)
    s = src.rearrange("p c t (a i) -> p c a t i", i=4)
    cut = nv // 4
    if nv > 0:
        nc.vector.tensor_copy(out=d[:, :, 0:cut], in_=s[:, :, 0:cut])
    if nv < P:
        nc.scalar.copy(out=d[:, :, cut:], in_=s[:, :, cut:])


def regroup_w4(copy, dst, src):
    copy(
        out=dst.rearrange("p t (a b) j -> p a j t b", b=MH),
        in_=src.rearrange("p j (a b t) -> p a j t b", b=MH, t=4),
    )


def tile_additivecoupling_pa_kernel(tc, x, h3, W4, b4, W5, b5, out):
    nc = tc.nc
    with ExitStack() as ctx:
        const = ctx.enter_context(tc.tile_pool(name="const", bufs=1))
        keep = ctx.enter_context(tc.tile_pool(name="keep", bufs=1))
        raw8 = ctx.enter_context(tc.tile_pool(name="raw8", bufs=3))
        raw4 = ctx.enter_context(tc.tile_pool(name="raw4", bufs=6))
        grp = ctx.enter_context(tc.tile_pool(name="grp", bufs=3))
        cod4 = ctx.enter_context(tc.tile_pool(name="cod4", bufs=4))
        h4pool = ctx.enter_context(tc.tile_pool(name="h4pool", bufs=2))
        opool = ctx.enter_context(tc.tile_pool(name="opool", bufs=8))
        psa = ctx.enter_context(tc.psum_pool(name="psa", bufs=8))

        ident = const.tile([P, P], F32, name="ident")
        make_identity(nc, ident[:])
        ctx.enter_context(tc.manual_schedule())
        brow = const.tile([P, 512], BF16, name="brow")
        nc.vector.memset(brow[:], 0.0)
        identb = const.tile([P, P], BF16, name="identb")
        nc.vector.tensor_copy(out=identb[:], in_=ident[:])

        raw = {}

        def load_w4_pair(g):
            r = raw8.tile([P, 4, 2 * KP], BF16, name="w4d", tag="w4d")
            nc.sync.dma_start(
                out=r[:], in_=W4[g * KP : (g + 1) * KP, 0 : 2 * KP].rearrange("(p j) c -> p j c", j=4)
            )
            raw[g] = r[:, :, 0:KP]
            raw[NG + g] = r[:, :, KP : 2 * KP]

        def load_w4(i):
            c2, g = divmod(i, NG)
            r = raw4.tile([P, 4, KP], BF16, name="w4r", tag="w4r")
            nc.sync.dma_start(
                out=r[:],
                in_=W4[g * KP : (g + 1) * KP, c2 * KP : (c2 + 1) * KP].rearrange("(p j) c -> p j c", j=4),
            )
            raw[i] = r[:]

        for i in reversed(PAIRS[0]):
            load_w4(i)
        h3r = []
        for bt in range(NBT):
            t_ = keep.tile([P, MID], BF16, name="h3r%d" % bt)
            nc.sync.dma_start(out=t_[:], in_=h3[bt * P : (bt + 1) * P, :])
            h3r.append(t_)
        nc.sync.dma_start(out=brow[0:4, :], in_=b4.rearrange("(r c) -> r c", c=512))
        nc.sync.dma_start(out=brow[4:5, :], in_=b5.rearrange("(r c) -> r c", c=512))
        for g in range(1, NG):
            load_w4_pair(g)
        for q in range(NG, len(PAIRS)):
            for i in reversed(PAIRS[q]):
                load_w4(i)
        raw5 = keep.tile([P, NG, 4, HALF], BF16, name="raw5")
        for c in range(NG):
            nc.sync.dma_start(
                out=raw5[:, c], in_=W5[c * KP : (c + 1) * KP, :].rearrange("(p t) j -> p t j", t=4)
            )
        xr = []
        for bt in range(NBT):
            t_ = keep.tile([P, 2 * HALF], BF16, name="xr%d" % bt)
            nc.sync.dma_start(out=t_[:], in_=x[bt * P : (bt + 1) * P, :])
            xr.append(t_)

        h3g = keep.tile([P, NG, B, 2], F32, name="h3g", align_bytes=64)
        h3c = keep.tile([P, NG, B], U32, name="h3c", align_bytes=64)
        h3s = keep.tile([P, NG, B], U8, name="h3s", align_bytes=64)

        def turn_h3(bt):
            words = h3r[bt][:].bitcast(F32)
            for gp in range(2):
                pt = psa.tile([P, 2, 2, P], F32, name="pt", tag="a")
                for gg in range(2):
                    for u in range(2):
                        w0 = (2 * gp + gg) * 256
                        nc.tensor.transpose(pt[:, gg, u, :], words[:, w0 + u : w0 + 256 : 2], ident[:])
                dst = h3g[:, 2 * gp : 2 * gp + 2, bt * P : (bt + 1) * P, :]
                src = pt[:].rearrange("p g u b -> p g b u")
                if gp == 0:
                    nc.scalar.copy(out=dst, in_=src)
                else:
                    nc.vector.tensor_copy(out=dst, in_=src)

        def quant_h3(g):
            nc.vector.quantize_mx(
                out=h3c[:, g, :].bitcast(FP8X4),
                scales=h3s[:, g, :],
                in_=h3g[:, g, :, :].rearrange("p b u -> p (b u)").bitcast(BF16),
            )

        grouped = {}
        codes = {}
        ps1 = {}
        h4g = {}
        h4c = [keep.tile([P, B], U32, name="h4c%d" % c, align_bytes=64) for c in range(NG)]
        h4s = [keep.tile([P, B], U8, name="h4s%d" % c, align_bytes=64) for c in range(NG)]
        w5c = [keep.tile([P, NG, P], U32, name="w5c%d" % jt, align_bytes=64) for jt in range(4)]
        w5s = [keep.tile([P, NG, P], U8, name="w5s%d" % jt, align_bytes=64) for jt in range(4)]

        def group_pair(q):
            g_ = grp.tile([P, 2, 4, P, 4], BF16, name="wg", tag="g", align_bytes=64)
            regroup_w4(nc.vector.tensor_copy, g_[:, 0], raw[PAIRS[q][0]])
            regroup_w4(nc.scalar.copy, g_[:, 1], raw[PAIRS[q][1]])
            grouped[q] = g_

        def quant_pair(q):
            cd = cod4.tile([P, 2, KP], U32, name="w4c", tag="w4c", align_bytes=64)
            sc = cod4.tile([P, 2, KP], U8, name="w4s", tag="w4s", align_bytes=64)
            nc.vector.quantize_mx(
                out=cd[:].rearrange("p u c -> p (u c)").bitcast(FP8X4),
                scales=sc[:].rearrange("p u c -> p (u c)"),
                in_=grouped[q][:].rearrange("p u t m j -> p (u t m j)"),
            )
            for u in range(2):
                codes[PAIRS[q][u]] = cd[:, u, :], sc[:, u, :]

        grouped5 = {}

        def group_w5(jt):
            g_ = grp.tile([P, NG, P, 4], BF16, name="wg5", tag="g5", align_bytes=64)
            regroup_w5(nc, g_, raw5[:, :, :, jt * P : (jt + 1) * P], NV_W5[jt])
            grouped5[jt] = g_

        def quant_w5(jt):
            nc.vector.quantize_mx(
                out=w5c[jt][:].rearrange("p c j -> p (c j)").bitcast(FP8X4),
                scales=w5s[jt][:].rearrange("p c j -> p (c j)"),
                in_=grouped5[jt][:].rearrange("p c j t -> p (c j t)"),
            )

        def layer1(i):
            g = i % NG
            cd, sc = codes[i]
            for t in range(4):
                if g == 0:
                    ps1[i // NG, t] = psa.tile([P, B], F32, name="ps1", tag="a")
                nc.tensor.matmul_mx(
                    out=ps1[i // NG, t][:],
                    lhsT=cd[:, t * P : (t + 1) * P].bitcast(FP8X4),
                    lhsT_scale=sc[:, t * P : (t + 1) * P],
                    rhs=h3c[:, g, :].bitcast(FP8X4),
                    rhs_scale=h3s[:, g, :],
                    start=(g == 0),
                    stop=(g == NG - 1),
                )

        h4p = {}

        def relu_h4(c2, ts, engine):
            if c2 not in h4p:
                h4p[c2] = h4pool.tile([P, 4, B], BF16, name="h4p", tag="h4p")
            for t in ts:
                dst, src, col = h4p[c2][:, t, :], ps1[c2, t][:], bias[:, c2, t : t + 1]
                if engine == "vector":
                    nc.vector.tensor_scalar(out=dst, in0=src, scalar1=col, scalar2=0.0, op0=ALU.add, op1=ALU.max)
                else:
                    nc.scalar.activation(out=dst, in_=src, func=ACT.Relu, bias=col, scale=1.0)

        def group_h4(c2, nv):
            hg = h4pool.tile([P, B, 4], BF16, name="h4g", tag="h4g", align_bytes=64)
            regroup_h4(nc, hg, h4p[c2], nv)
            h4g[c2] = hg

        def quant_h4(c2):
            nc.vector.quantize_mx(
                out=h4c[c2][:].bitcast(FP8X4),
                scales=h4s[c2][:],
                in_=h4g[c2][:].rearrange("p b t -> p (b t)"),
            )

        acc = {}

        def layer2(jt, cs):
            for c in cs:
                if c == 0:
                    acc[jt] = psa.tile([P, B], F32, name="acc", tag="a")
                nc.tensor.matmul_mx(
                    out=acc[jt][:],
                    lhsT=w5c[jt][:, c, :].bitcast(FP8X4),
                    lhsT_scale=w5s[jt][:, c, :],
                    rhs=h4c[c][:].bitcast(FP8X4),
                    rhs_scale=h4s[c][:],
                    start=(c == 0),
                    stop=(c == NG - 1),
                )

        zt = {}

        def add_b5(jt):
            z = keep.tile([P, B], F32, name="zt%d" % jt)
            col = bias5[:, jt : jt + 1]
            if jt % 2 == 0:
                nc.scalar.activation(out=z[:], in_=acc[jt][:], func=ACT.Identity, bias=col, scale=1.0)
            else:
                nc.vector.tensor_scalar(out=z[:], in0=acc[jt][:], scalar1=col, scalar2=None, op0=ALU.add)
            zt[jt] = z

        fin = {}

        def add_x(bt, half):
            f = psa.tile([P, 2, 2 * P], F32, name="f", tag="a")
            nc.tensor.matmul(
                out=f[:],
                lhsT=identb[:],
                rhs=xr[bt][:, half * HALF : (half + 1) * HALF].rearrange("p (j e) -> p e j", e=2),
                start=True,
                stop=False,
            )
            fin[bt, half] = f

        def add_m(bt, half):
            for r in range(2):
                nc.tensor.matmul(
                    out=fin[bt, half][:, 0, r * P : (r + 1) * P],
                    lhsT=zt[2 * half + r][:, bt * P : (bt + 1) * P],
                    rhs=ident[:],
                    is_transpose=True,
                    start=False,
                    stop=(r == 1),
                )

        def store(bt, half):
            o = opool.tile([P, 2 * P, 2], F32, name="o", tag="o")
            src = fin[bt, half][:].rearrange("p e j -> p j e")
            if bt % 2 == 0:
                nc.scalar.copy(out=o[:], in_=src)
            else:
                nc.vector.tensor_copy(out=o[:], in_=src)
            nc.sync.dma_start(
                out=out[bt * P : (bt + 1) * P, half * HALF : (half + 1) * HALF],
                in_=o[:].rearrange("p j e -> p (j e)"),
            )

        group_pair(0)
        turn_h3(0)
        quant_pair(0)
        for bt in range(1, NBT):
            turn_h3(bt)
        browf = const.tile([P, 512], F32, name="browf")
        nc.vector.tensor_copy(out=browf[:], in_=brow[:])
        group_pair(1)
        quant_h3(0)
        pb = psa.tile([P, 4, P], F32, name="pb", tag="a")
        pb5 = psa.tile([P, 4, P], F32, name="pb5", tag="a")
        for t in range(4):
            nc.tensor.transpose(pb[:, t, :], browf[:, t : 512 : 4], ident[:])
        for t in range(4):
            nc.tensor.transpose(pb5[:, t, :], browf[:, t * P : (t + 1) * P], ident[:])
        quant_h3(1)
        quant_h3(2)
        quant_h3(3)
        bias = const.tile([P, 4, 4], F32, name="bias")
        nc.vector.tensor_copy(out=bias[:], in_=pb[:, :, 0:4].rearrange("p t c -> p c t"))
        bias5 = const.tile([P, 4], F32, name="bias5")
        nc.vector.tensor_copy(out=bias5[:], in_=pb5[:, :, 4])
        for i in PAIRS[0]:
            layer1(i)

        for q in range(1, len(PAIRS)):
            if q + 1 < len(PAIRS):
                group_pair(q + 1)
            else:
                group_w5(0)
            if q in RELU_STEP:
                relu_h4(RELU_STEP[q], range(4), "scalar")
            quant_pair(q)
            for i in PAIRS[q]:
                layer1(i)
            if q - 1 in RELU_STEP:
                group_h4(RELU_STEP[q - 1], B)
            if q - 2 in RELU_STEP:
                quant_h4(RELU_STEP[q - 2])

        group_w5(1)
        quant_w5(0)
        group_h4(2, B)
        group_w5(2)
        quant_h4(2)
        quant_w5(1)
        relu_h4(3, range(4), "scalar")
        layer2(0, (0, 1, 2))
        layer2(1, (0, 1, 2))
        quant_w5(2)
        group_h4(3, 320)
        for bt in range(NBT):
            add_x(bt, 0)
        quant_h4(3)
        layer2(0, (3,))
        layer2(1, (3,))
        layer2(2, (0, 1, 2, 3))
        group_w5(3)
        add_b5(0)
        add_b5(1)
        for bt in range(NBT):
            add_m(bt, 0)
        quant_w5(3)
        layer2(3, (0, 1, 2, 3))
        store(0, 0)
        store(1, 0)
        add_b5(2)
        store(2, 0)
        store(3, 0)
        for bt in range(NBT):
            add_x(bt, 1)
        add_b5(3)
        for bt in range(NBT):
            add_m(bt, 1)
        for bt in range(NBT):
            store(bt, 1)
